import numpy as np
import ml_dtypes


def mxq(x, axis, fmt="e4m3"):
    dtype, down = {"e4m3": (ml_dtypes.float8_e4m3fn, 7), "e5m2": (ml_dtypes.float8_e5m2, 14)}[fmt]
    v = np.moveaxis(np.asarray(x, np.float32).astype(ml_dtypes.bfloat16).astype(np.float64), axis, -1)
    blocks = v.reshape(v.shape[:-1] + (-1, 32))
    amax = np.abs(blocks).max(-1, keepdims=True)
    byte = np.maximum(np.where(amax > 0, np.frexp(amax)[1] - 1 + 127, 0) - down, 1)
    scale = np.exp2(byte - 127.0)
    codes = (blocks / scale).astype(np.float32).astype(dtype).astype(np.float64)
    return np.moveaxis((codes * scale).reshape(v.shape), -1, axis)


WIDE = False


def mx_kscale(k):
    if not WIDE:
        return np.ones(k)
    levels = np.array([10, -10, 5, -5, 0])
    a = np.random.permutation(np.resize(levels, k // 512 * 4)).reshape(k // 512, 4)
    idx = np.arange(k)
    return np.exp2(a[idx // 512, idx % 128 // 32])


BF16 = ml_dtypes.bfloat16


def bf(x):
    return np.asarray(x, np.float32).astype(BF16)


def f64(x):
    return np.asarray(x).astype(np.float64)


B, S, H, HEAD_DIM, ROPE_DIM, RATIO = 8, 1024, 512, 128, 64, 32
ROPE_THETA = 10000.0
NEG = -1e9


def rotate_half_interleaved(x):
    x1 = x[..., 0::2]
    x2 = x[..., 1::2]
    return np.stack([-x2, x1], axis=-1).reshape(x.shape)


def softmax(v, axis):
    e = np.exp(v - v.max(axis=axis, keepdims=True))
    return e / e.sum(axis=axis, keepdims=True)


def setup_inputs():
    s = mx_kscale(H)
    return {"hidden_states": bf(np.random.standard_normal((B, S, H)) * s),
            "w_kv": bf(np.random.standard_normal((H, 2 * HEAD_DIM)) * 2.0 / np.sqrt(H) / s[:, None]),
            "w_gate": bf(np.random.standard_normal((H, 2 * HEAD_DIM)) * 1.0 / np.sqrt(H) / s[:, None]),
            "position_bias": bf(np.random.standard_normal((2 * RATIO, HEAD_DIM)) * 0.5)}


def reference(hidden_states, w_kv, w_gate, position_bias):
    d, r = HEAD_DIM, RATIO
    n = S // r
    hq = mxq(f64(hidden_states), 2, "e4m3")
    kv = hq @ mxq(f64(w_kv), 0, "e4m3")
    gate = hq @ mxq(f64(w_gate), 0, "e4m3")

    chunk_kv = kv[:, : n * r].reshape(B, n, r, 2 * d)
    chunk_gate = gate[:, : n * r].reshape(B, n, r, 2 * d)

    kv_lo, kv_hi = chunk_kv[..., :d], chunk_kv[..., d:]
    g_lo, g_hi = chunk_gate[..., :d], chunk_gate[..., d:]
    prev_kv = np.concatenate([np.zeros_like(kv_lo[:, :1]), kv_lo[:, :-1]], axis=1)
    prev_g = np.concatenate([np.full_like(g_lo[:, :1], NEG), g_lo[:, :-1]], axis=1)
    win_kv = np.concatenate([prev_kv, kv_hi], axis=2)
    win_g = np.concatenate([prev_g, g_hi], axis=2)

    w = softmax(win_g + f64(position_bias)[None, None], 2)
    pooled = np.sum(w * win_kv, axis=2)

    positions = np.arange(n, dtype=np.float64) * r
    inv_freq = 1.0 / (ROPE_THETA ** (np.arange(0, ROPE_DIM, 2, dtype=np.float64) / ROPE_DIM))
    freqs = positions[:, None] * inv_freq[None, :]
    cos = np.repeat(np.cos(freqs), 2, axis=-1)
    sin = np.repeat(np.sin(freqs), 2, axis=-1)

    nope, rope = pooled[..., :-ROPE_DIM], pooled[..., -ROPE_DIM:]
    rotated = rope * cos[None] + rotate_half_interleaved(rope) * sin[None]
    return np.concatenate([nope, rotated], axis=-1)

@@ -1,0 +1,323 @@
+from contextlib import ExitStack
+
+import concourse.mybir as mybir
+from concourse.masks import make_identity
+
+F32 = mybir.dt.float32
+BF16 = mybir.dt.bfloat16
+I32 = mybir.dt.int32
+U32 = mybir.dt.uint32
+U8 = mybir.dt.uint8
+FP8X4 = mybir.dt.float8_e4m3fn_x4
+ALU = mybir.AluOpType
+ACT = mybir.ActivationFunctionType
+AX = mybir.AxisListType
+
+FLOPS = 2 * 8192 * 512 * 512
+
+P = 128
+NG = 16
+NEG = -1.0e9
+MANUAL = False
+
+INV2PI = 0.15915493667125702
+TWO_PI_1 = 6.28125
+TWO_PI_2 = 0.0019352436065673828
+TWO_PI_3 = 6.357301884918343e-08
+HALF_PI_1 = 1.5707963705062866
+HALF_PI_2 = -4.371138828673793e-08
+
+
+def tile_deepseekv4csacompressor_t_kernel(tc, hidden_states, w_kv, w_gate, position_bias, out):
+    nc = tc.nc
+    with ExitStack() as ctx:
+        const = ctx.enter_context(tc.tile_pool(name="const", bufs=1))
+        xin = ctx.enter_context(tc.tile_pool(name="xin", bufs=1))
+        twp = ctx.enter_context(tc.tile_pool(name="twp", bufs=1))
+        gpool = ctx.enter_context(tc.tile_pool(name="gpool", bufs=3))
+        cpool = ctx.enter_context(tc.tile_pool(name="cpool", bufs=4))
+        sm = ctx.enter_context(tc.tile_pool(name="sm", bufs=2))
+        xtp = ctx.enter_context(tc.psum_pool(name="xtp", bufs=2))
+        gp = ctx.enter_context(tc.psum_pool(name="gp", bufs=2))
+        kp = ctx.enter_context(tc.psum_pool(name="kp", bufs=2))
+        mp = ctx.enter_context(tc.psum_pool(name="mp", bufs=2))
+        if MANUAL:
+            ctx.enter_context(tc.manual_schedule())
+
+        hid = hidden_states.rearrange("b s h -> (b s) h").rearrange("(g a p) h -> g p a h", a=4, p=P)
+        outr = out.rearrange("b i c -> (b i) c")
+
+        xs = []
+
+        def load_x(g):
+            x = xin.tile([P, 4, 512], BF16, name="x%d" % g)
+            if g == 0:
+                nc.sync.dma_start(out=x[:, 0:2, :], in_=hid[g][:, 0:2, :])
+                nc.sync.dma_start(out=x[:, 2:4, :], in_=hid[g][:, 2:4, :])
+            else:
+                nc.sync.dma_start(out=x[:], in_=hid[g])
+            xs.append(x)
+
+        load_x(0)
+        raws = []
+        for nm, w in (("kv", w_kv), ("gate", w_gate)):
+            raws.append(const.tile([P, 4, 256], BF16, name="raw_%s" % nm))
+        for i, w in ((1, w_gate), (0, w_kv)):
+            nc.sync.dma_start(
+                out=raws[i][:].rearrange("q (u e) n -> q u (e n)", u=2),
+                in_=w.rearrange("(u q e) n -> q u (e n)", u=2, e=2),
+            )
+        for g in range(1, NG):
+            load_x(g)
+
+        ident = const.tile([P, P], F32, name="ident")
+        make_identity(nc, ident[:])
+
+        bz = const.tile([P, P], BF16, name="bz")
+        nc.vector.memset(bz[64:128, :], 0.0)
+        nc.scalar.dma_start(out=bz[0:64, :], in_=position_bias)
+
+        tw = []
+        for g in range(NG):
+            tw.append(twp.tile([P, 16, 64], F32, name="tw%d" % g))
+        for g in range(0, NG, 2):
+            nc.gpsimd.memset(tw[g][:, 0, 0:32], NEG)
+        den = []
+        num = []
+        for h in range(2):
+            den.append(const.tile([P, P], F32, name="den%d" % h))
+            num.append(const.tile([P, P], F32, name="num%d" % h))
+
+        def small(nm, dt=F32, w=32):
+            return const.tile([P, w], dt, name=nm)
+
+        pidx = small("pidx", I32, 1)
+        nc.gpsimd.iota(pidx[:], pattern=[[0, 1]], base=0, channel_multiplier=1)
+        posi = small("posi", I32, 1)
+        nc.vector.tensor_scalar(
+            out=posi[:], in0=pidx[:], scalar1=31, scalar2=5, op0=ALU.bitwise_and, op1=ALU.logical_shift_left
+        )
+        posf = small("posf", F32, 1)
+        nc.vector.tensor_copy(out=posf[:], in_=posi[:])
+        ang = small("ang")
+        for j in range(32):
+            nc.vector.tensor_scalar(
+                out=ang[:, j:j + 1], in0=posf[:, 0:1], scalar1=10000.0 ** (-j / 32.0), scalar2=None, op0=ALU.mult
+            )
+        xk = small("xk")
+        nc.vector.tensor_scalar(out=xk[:], in0=ang[:], scalar1=INV2PI, scalar2=None, op0=ALU.mult)
+        kc = small("kc", I32)
+        nc.vector.tensor_copy(out=kc[:], in_=xk[:])
+        ki = small("ki", I32)
+        nc.vector.tensor_single_scalar(out=ki[:], in_=kc[:], scalar=255, op=ALU.bitwise_and)
+        kf = small("kf")
+        nc.vector.tensor_copy(out=kf[:], in_=ki[:])
+        r_prev = ang
+        for n, c in enumerate((TWO_PI_1, TWO_PI_2, TWO_PI_3)):
+            r = small("r%d" % n)
+            nc.vector.scalar_tensor_tensor(out=r[:], in0=kf[:], scalar=-c, in1=r_prev[:], op0=ALU.mult, op1=ALU.add)
+            r_prev = r
+        ab = small("ab")
+        nc.vector.scalar_tensor_tensor(out=ab[:], in0=r_prev[:], scalar=-1.0, in1=r_prev[:], op0=ALU.mult, op1=ALU.max)
+        uu = small("uu")
+        nc.vector.tensor_scalar(out=uu[:], in0=ab[:], scalar1=-HALF_PI_1, scalar2=-HALF_PI_2, op0=ALU.add, op1=ALU.add)
+        ss = const.tile([P, 32, 2], F32, name="ss")
+        cosT = small("cosT")
+        nc.scalar.activation(out=ss[:, :, 1], in_=r_prev[:], func=ACT.Sin)
+        nc.scalar.activation(out=ss[:, :, 0], in_=r_prev[:], func=ACT.Sin, scale=-1.0)
+        nc.scalar.activation(out=cosT[:], in_=uu[:], func=ACT.Sin, scale=-1.0)
+
+        wgrp = const.tile([P, 512, 4], BF16, name="wgrp", align_bytes=64)
+        wcodes = const.tile([P, 512], U32, name="wcodes", align_bytes=64)
+        wscl = const.tile([P, 512], U8, name="wscl", align_bytes=64)
+        def w_regroup(i):
+            cols = slice(256 * i, 256 * i + 256)
+            nc.vector.tensor_copy(out=wgrp[:, cols, :], in_=raws[i][:].rearrange("q t n -> q n t"))
+
+        def w_quantise(i):
+            cols = slice(256 * i, 256 * i + 256)
+            nc.vector.quantize_mx(
+                out=wcodes[:, cols].bitcast(FP8X4),
+                scales=wscl[:, cols],
+                in_=wgrp[:, cols, :].rearrange("q n t -> q (n t)"),
+            )
+
+        bzf = const.tile([P, P], F32, name="bzf")
+        nc.vector.tensor_copy(out=bzf[:], in_=bz[:])
+        bT = mp.tile([P, P], F32, name="bT", tag="misc")
+        nc.tensor.transpose(bT[:], bzf[:], ident[:])
+        w_regroup(1)
+        bias = const.tile([P, 64], F32, name="bias")
+        nc.vector.tensor_copy(out=bias[:], in_=bT[:, 0:64])
+        w_quantise(1)
+
+        st = {}
+
+        def transposes(g):
+            xw = xs[g][:].bitcast(F32)
+            tiles = []
+            for hf in range(2):
+                xt = xtp.tile([P, 2, 2, P], F32, name="xt")
+                for a in range(2):
+                    for u in range(2):
+                        nc.tensor.transpose(xt[:, a, u, :], xw[:, 2 * hf + a, 128 * u:128 * u + 128], ident[:])
+                tiles.append(xt)
+            st[("xt", g)] = tiles
+
+        def evac(g):
+            grp = gpool.tile([P, 2048], BF16, name="grp", align_bytes=64)
+            gw = grp[:].bitcast(F32).rearrange("q (a p u) -> q a p u", a=4, u=2)
+            for hf in range(2):
+                nc.scalar.copy(
+                    out=gw[:, 2 * hf:2 * hf + 2, :, :],
+                    in_=st[("xt", g)][hf][:].rearrange("q a u p -> q a p u"),
+                )
+            st[("grp", g)] = grp
+
+        def quantise(g):
+            codes = cpool.tile([P, 512], U32, name="codes", align_bytes=64)
+            scl = cpool.tile([P, 512], U8, name="scl", align_bytes=64)
+            nc.vector.quantize_mx(out=codes[:].bitcast(FP8X4), scales=scl[:], in_=st[("grp", g)][:])
+            st[("q", g)] = (codes, scl)
+
+        def mx(pool, nm, g, m):
+            codes, scl = st[("q", g)]
+            ps = pool.tile([P, 512], F32, name=nm)
+            nc.tensor.matmul_mx(
+                out=ps[:],
+                lhsT=wcodes[:, 128 * m:128 * m + 128].bitcast(FP8X4),
+                lhsT_scale=wscl[:, 128 * m:128 * m + 128],
+                rhs=codes[:].bitcast(FP8X4),
+                rhs_scale=scl[:],
+                start=True,
+                stop=True,
+            )
+            return ps
+
+        def gate_mm(g):
+            st[("g", g)] = (mx(gp, "gps", g, 2), mx(gp, "gps", g, 3))
+
+        def kv_mm(g):
+            st[("kv", g)] = (mx(kp, "kps", g, 0), mx(kp, "kps", g, 1))
+
+        def bias_add(g):
+            glo, ghi = st[("g", g)]
+            nc.vector.tensor_tensor(
+                out=tw[g][:, 1:16, 0:32],
+                in0=glo[:, 0:480].rearrange("c (j s) -> c j s", s=32),
+                in1=bias[:, 0:32].unsqueeze(1).to_broadcast([P, 15, 32]),
+                op=ALU.add,
+            )
+            if g % 2 == 0:
+                nc.vector.tensor_tensor(out=tw[g + 1][:, 0, 0:32], in0=glo[:, 480:512], in1=bias[:, 0:32], op=ALU.add)
+            nc.vector.tensor_tensor(
+                out=tw[g][:, :, 32:64],
+                in0=ghi[:].rearrange("c (j s) -> c j s", s=32),
+                in1=bias[:, 32:64].unsqueeze(1).to_broadcast([P, 16, 32]),
+                op=ALU.add,
+            )
+
+        def window_max(g):
+            negm = sm.tile([P, 16], F32, name="negm", bufs=3)
+            nc.vector.tensor_reduce(out=negm[:], in_=tw[g][:], axis=AX.X, op=ALU.max, negate=True)
+            st[("negm", g)] = negm
+
+        def exps(g):
+            negm = st[("negm", g)]
+            h, c0 = g // 8, 16 * (g % 8)
+            for w in range(16):
+                nc.scalar.activation(
+                    out=tw[g][:, w, :],
+                    in_=tw[g][:, w, :],
+                    func=ACT.Exp,
+                    bias=negm[:, w:w + 1],
+                    scale=1.0,
+                    accum_out=den[h][:, c0 + w:c0 + w + 1],
+                )
+
+        def weigh(g):
+            klo, khi = st[("kv", g)]
+            nc.vector.tensor_tensor(
+                out=tw[g][:, 1:16, 0:32],
+                in0=tw[g][:, 1:16, 0:32],
+                in1=klo[:, 0:480].rearrange("c (j s) -> c j s", s=32),
+                op=ALU.mult,
+            )
+            if g % 2 == 0:
+                kvs = sm.tile([P, 32], F32, name="kvs")
+                nc.vector.tensor_copy(out=kvs[:], in_=klo[:, 480:512])
+                st[("kvs", g)] = kvs
+            else:
+                nc.vector.tensor_tensor(
+                    out=tw[g][:, 0, 0:32], in0=tw[g][:, 0, 0:32], in1=st[("kvs", g - 1)][:], op=ALU.mult
+                )
+            nc.vector.tensor_tensor(
+                out=tw[g][:, :, 32:64],
+                in0=tw[g][:, :, 32:64],
+                in1=khi[:].rearrange("c (j s) -> c j s", s=32),
+                op=ALU.mult,
+            )
+
+        def pool_sum(g):
+            h, c0 = g // 8, 16 * (g % 8)
+            if g == NG - 1:
+                nc.vector.tensor_reduce(out=num[h][:, c0:c0 + 16], in_=tw[g][:], axis=AX.X, op=ALU.add)
+                return
+            n = 32
+            while n > 1:
+                nc.gpsimd.tensor_tensor(out=tw[g][:, :, 0:n], in0=tw[g][:, :, 0:n], in1=tw[g][:, :, n:2 * n], op=ALU.add)
+                n = n // 2
+            nc.gpsimd.tensor_tensor(out=num[h][:, c0:c0 + 16], in0=tw[g][:, :, 0], in1=tw[g][:, :, 1], op=ALU.add)
+
+        def final(h):
+            rden = sm.tile([P, P], F32, name="rden")
+            nc.vector.reciprocal(out=rden[:], in_=den[h][:])
+            pooled = sm.tile([P, P], F32, name="pooled")
+            nc.vector.tensor_tensor(out=pooled[:], in0=num[h][:], in1=rden[:], op=ALU.mult)
+            pt = mp.tile([P, P], F32, name="pt", tag="misc")
+            nc.tensor.transpose(pt[:], pooled[:], ident[:])
+            o = sm.tile([P, P], F32, name="o")
+            nc.vector.tensor_copy(out=o[:, 0:64], in_=pt[:, 0:64])
+            xr = pt[:, 64:128].rearrange("w (j e) -> w j e", e=2)
+            y = sm.tile([P, 32, 2], F32, name="y")
+            nc.vector.tensor_tensor(out=y[:], in0=xr, in1=cosT[:].unsqueeze(2).to_broadcast([P, 32, 2]), op=ALU.mult)
+            z = sm.tile([P, 32, 2], F32, name="z")
+            nc.vector.tensor_tensor(out=z[:, :, 0], in0=xr[:, :, 1], in1=ss[:, :, 0], op=ALU.mult)
+            nc.vector.tensor_tensor(out=z[:, :, 1], in0=xr[:, :, 0], in1=ss[:, :, 1], op=ALU.mult)
+            nc.vector.tensor_tensor(
+                out=o[:, 64:128].rearrange("w (j e) -> w j e", e=2), in0=y[:], in1=z[:], op=ALU.add
+            )
+            nc.sync.dma_start(out=outr[128 * h:128 * h + 128, :], in_=o[:])
+
+        def on(g):
+            return 0 <= g < NG
+
+        ctx.enter_context(tc.manual_schedule())
+        for k in range(-2, NG + 2):
+            if on(k + 2):
+                transposes(k + 2)
+            if on(k):
+                bias_add(k)
+            if on(k + 1):
+                quantise(k + 1)
+            if k == -1:
+                w_regroup(0)
+            if k == 0:
+                w_quantise(0)
+            if on(k + 2):
+                evac(k + 2)
+            if on(k):
+                window_max(k)
+            if on(k + 1):
+                gate_mm(k + 1)
+            if on(k):
+                exps(k)
+            if on(k - 1):
+                weigh(k - 1)
+            if on(k):
+                kv_mm(k)
+            if on(k - 1):
+                pool_sum(k - 1)
+            if k == NG - 1:
+                final(0)
+        final(1)

@@ -18,7 +18,8 @@ FLOPS = 2 * 8192 * 512 * 512
 P = 128
 NG = 16
 NEG = -1.0e9
-MANUAL = False
+OFFLOAD = False
+LEFT = 8
 
 INV2PI = 0.15915493667125702
 TWO_PI_1 = 6.28125
@@ -39,10 +40,8 @@ def tile_deepseekv4csacompressor_t_kernel(tc, hidden_states, w_kv, w_gate, posit
         sm = ctx.enter_context(tc.tile_pool(name="sm", bufs=2))
         xtp = ctx.enter_context(tc.psum_pool(name="xtp", bufs=2))
         gp = ctx.enter_context(tc.psum_pool(name="gp", bufs=2))
-        kp = ctx.enter_context(tc.psum_pool(name="kp", bufs=2))
-        mp = ctx.enter_context(tc.psum_pool(name="mp", bufs=2))
-        if MANUAL:
-            ctx.enter_context(tc.manual_schedule())
+        kp = ctx.enter_context(tc.psum_pool(name="kp", bufs=1))
+        mp = ctx.enter_context(tc.psum_pool(name="mp", bufs=1))
 
         hid = hidden_states.rearrange("b s h -> (b s) h").rearrange("(g a p) h -> g p a h", a=4, p=P)
         outr = out.rearrange("b i c -> (b i) c")
@@ -60,7 +59,7 @@ def tile_deepseekv4csacompressor_t_kernel(tc, hidden_states, w_kv, w_gate, posit
 
         load_x(0)
         raws = []
-        for nm, w in (("kv", w_kv), ("gate", w_gate)):
+        for nm in ("kv", "gate"):
             raws.append(const.tile([P, 4, 256], BF16, name="raw_%s" % nm))
         for i, w in ((1, w_gate), (0, w_kv)):
             nc.sync.dma_start(
@@ -77,11 +76,10 @@ def tile_deepseekv4csacompressor_t_kernel(tc, hidden_states, w_kv, w_gate, posit
         nc.vector.memset(bz[64:128, :], 0.0)
         nc.scalar.dma_start(out=bz[0:64, :], in_=position_bias)
 
-        tw = []
-        for g in range(NG):
-            tw.append(twp.tile([P, 16, 64], F32, name="tw%d" % g))
-        for g in range(0, NG, 2):
-            nc.gpsimd.memset(tw[g][:, 0, 0:32], NEG)
+        tb = []
+        for b in range(NG // 2):
+            tb.append(twp.tile([P, 32, 64], F32, name="tb%d" % b))
+            nc.gpsimd.memset(tb[b][:, 0, 0:32], NEG)
         den = []
         num = []
         for h in range(2):
@@ -130,6 +128,7 @@ def tile_deepseekv4csacompressor_t_kernel(tc, hidden_states, w_kv, w_gate, posit
         wgrp = const.tile([P, 512, 4], BF16, name="wgrp", align_bytes=64)
         wcodes = const.tile([P, 512], U32, name="wcodes", align_bytes=64)
         wscl = const.tile([P, 512], U8, name="wscl", align_bytes=64)
+
         def w_regroup(i):
             cols = slice(256 * i, 256 * i + 256)
             nc.vector.tensor_copy(out=wgrp[:, cols, :], in_=raws[i][:].rearrange("q t n -> q n t"))
@@ -152,6 +151,9 @@ def tile_deepseekv4csacompressor_t_kernel(tc, hidden_states, w_kv, w_gate, posit
         w_quantise(1)
 
         st = {}
+
+        def chunks(ap):
+            return ap.rearrange("c (j s) -> c j s", s=32)
 
         def transposes(g):
             xw = xs[g][:].bitcast(F32)
@@ -180,102 +182,127 @@ def tile_deepseekv4csacompressor_t_kernel(tc, hidden_states, w_kv, w_gate, posit
             nc.vector.quantize_mx(out=codes[:].bitcast(FP8X4), scales=scl[:], in_=st[("grp", g)][:])
             st[("q", g)] = (codes, scl)
 
-        def mx(pool, nm, g, m):
+        def mx(pool, nm, g, m, c0, c1):
             codes, scl = st[("q", g)]
-            ps = pool.tile([P, 512], F32, name=nm)
+            ps = pool.tile([P, c1 - c0], F32, name=nm)
             nc.tensor.matmul_mx(
                 out=ps[:],
                 lhsT=wcodes[:, 128 * m:128 * m + 128].bitcast(FP8X4),
                 lhsT_scale=wscl[:, 128 * m:128 * m + 128],
-                rhs=codes[:].bitcast(FP8X4),
-                rhs_scale=scl[:],
+                rhs=codes[:, c0:c1].bitcast(FP8X4),
+                rhs_scale=scl[:, c0:c1],
                 start=True,
                 stop=True,
             )
             return ps
 
         def gate_mm(g):
-            st[("g", g)] = (mx(gp, "gps", g, 2), mx(gp, "gps", g, 3))
+            st[("g", g)] = (mx(gp, "gps", g, 2, 0, 512), mx(gp, "gps", g, 3, 0, 512))
 
         def kv_mm(g):
-            st[("kv", g)] = (mx(kp, "kps", g, 0), mx(kp, "kps", g, 1))
+            if OFFLOAD:
+                st[("kv", g)] = (
+                    mx(kp, "kla", g, 0, 0, 256), mx(kp, "khi", g, 1, 0, 512), mx(kp, "klb", g, 0, 256, 512)
+                )
+            else:
+                st[("kv", g)] = (mx(kp, "kla", g, 0, 0, 512), mx(kp, "khi", g, 1, 0, 512), None)
 
         def bias_add(g):
             glo, ghi = st[("g", g)]
+            t, w0 = tb[g // 2], 16 * (g % 2)
+            n = 16 - g % 2
             nc.vector.tensor_tensor(
-                out=tw[g][:, 1:16, 0:32],
-                in0=glo[:, 0:480].rearrange("c (j s) -> c j s", s=32),
-                in1=bias[:, 0:32].unsqueeze(1).to_broadcast([P, 15, 32]),
+                out=t[:, w0 + 1:w0 + 1 + n, 0:32],
+                in0=chunks(glo[:, 0:32 * n]),
+                in1=bias[:, 0:32].unsqueeze(1).to_broadcast([P, n, 32]),
                 op=ALU.add,
             )
-            if g % 2 == 0:
-                nc.vector.tensor_tensor(out=tw[g + 1][:, 0, 0:32], in0=glo[:, 480:512], in1=bias[:, 0:32], op=ALU.add)
             nc.vector.tensor_tensor(
-                out=tw[g][:, :, 32:64],
-                in0=ghi[:].rearrange("c (j s) -> c j s", s=32),
+                out=t[:, w0:w0 + 16, 32:64],
+                in0=chunks(ghi[:]),
                 in1=bias[:, 32:64].unsqueeze(1).to_broadcast([P, 16, 32]),
                 op=ALU.add,
             )
 
         def window_max(g):
+            t, w0 = tb[g // 2], 16 * (g % 2)
             negm = sm.tile([P, 16], F32, name="negm", bufs=3)
-            nc.vector.tensor_reduce(out=negm[:], in_=tw[g][:], axis=AX.X, op=ALU.max, negate=True)
+            nc.vector.tensor_reduce(out=negm[:], in_=t[:, w0:w0 + 16, :], axis=AX.X, op=ALU.max, negate=True)
             st[("negm", g)] = negm
 
         def exps(g):
+            t, w0 = tb[g // 2], 16 * (g % 2)
             negm = st[("negm", g)]
             h, c0 = g // 8, 16 * (g % 8)
             for w in range(16):
                 nc.scalar.activation(
-                    out=tw[g][:, w, :],
-                    in_=tw[g][:, w, :],
+                    out=t[:, w0 + w, :],
+                    in_=t[:, w0 + w, :],
                     func=ACT.Exp,
                     bias=negm[:, w:w + 1],
                     scale=1.0,
                     accum_out=den[h][:, c0 + w:c0 + w + 1],
                 )
 
+        def kv_evac(g):
+            kvb = sm.tile([P, 256], F32, name="kvb", bufs=3)
+            nc.scalar.copy(out=kvb[:], in_=st[("kv", g)][2][:])
+            st[("kvb", g)] = kvb
+
+        def mul(eng, view, other):
+            eng.tensor_tensor(out=view, in0=view, in1=other, op=ALU.mult)
+
         def weigh(g):
-            klo, khi = st[("kv", g)]
-            nc.vector.tensor_tensor(
-                out=tw[g][:, 1:16, 0:32],
-                in0=tw[g][:, 1:16, 0:32],
-                in1=klo[:, 0:480].rearrange("c (j s) -> c j s", s=32),
-                op=ALU.mult,
-            )
-            if g % 2 == 0:
-                kvs = sm.tile([P, 32], F32, name="kvs")
-                nc.vector.tensor_copy(out=kvs[:], in_=klo[:, 480:512])
-                st[("kvs", g)] = kvs
-            else:
-                nc.vector.tensor_tensor(
-                    out=tw[g][:, 0, 0:32], in0=tw[g][:, 0, 0:32], in1=st[("kvs", g - 1)][:], op=ALU.mult
-                )
-            nc.vector.tensor_tensor(
-                out=tw[g][:, :, 32:64],
-                in0=tw[g][:, :, 32:64],
-                in1=khi[:].rearrange("c (j s) -> c j s", s=32),
-                op=ALU.mult,
-            )
-
-        def pool_sum(g):
-            h, c0 = g // 8, 16 * (g % 8)
-            if g == NG - 1:
-                nc.vector.tensor_reduce(out=num[h][:, c0:c0 + 16], in_=tw[g][:], axis=AX.X, op=ALU.add)
+            kla, khi, klb = st[("kv", g)]
+            t, w0 = tb[g // 2], 16 * (g % 2)
+            if not OFFLOAD:
+                mul(nc.vector, t[:, w0 + 1:w0 + 16, 0:32], chunks(kla[:, 0:480]))
+                if g % 2 == 0:
+                    kvs = sm.tile([P, 32], F32, name="kvs")
+                    nc.vector.tensor_copy(out=kvs[:], in_=kla[:, 480:512])
+                    st[("kvs", g)] = kvs
+                else:
+                    mul(nc.vector, t[:, w0, 0:32], st[("kvs", g - 1)][:])
+                mul(nc.vector, t[:, w0:w0 + 16, 32:64], chunks(khi[:]))
                 return
-            n = 32
-            while n > 1:
-                nc.gpsimd.tensor_tensor(out=tw[g][:, :, 0:n], in0=tw[g][:, :, 0:n], in1=tw[g][:, :, n:2 * n], op=ALU.add)
-                n = n // 2
-            nc.gpsimd.tensor_tensor(out=num[h][:, c0:c0 + 16], in0=tw[g][:, :, 0], in1=tw[g][:, :, 1], op=ALU.add)
+            mul(nc.vector, t[:, w0 + 1:w0 + 9, 0:32], chunks(kla[:]))
+            mul(nc.vector, t[:, w0:w0 + 16, 32:64], chunks(khi[:]))
+            if g == NG - 1:
+                mul(nc.vector, t[:, w0 + 9:w0 + 16, 0:32], chunks(klb[:, 0:224]))
+                mul(nc.vector, t[:, w0, 0:32], st[("kvb", g - 1)][:, 224:256])
 
-        def final(h):
+        def weigh_late(g):
+            t, w0 = tb[g // 2], 16 * (g % 2)
+            mul(nc.gpsimd, t[:, w0 + 9:w0 + 16, 0:32], chunks(st[("kvb", g)][:, 0:224]))
+            if g % 2 == 1:
+                mul(nc.gpsimd, t[:, w0, 0:32], st[("kvb", g - 1)][:, 224:256])
+
+        def tree(g):
+            t, w0 = tb[g // 2], 16 * (g % 2)
+            n = 32
+            while n >= LEFT:
+                nc.gpsimd.tensor_tensor(
+                    out=t[:, w0:w0 + 16, 0:n], in0=t[:, w0:w0 + 16, 0:n], in1=t[:, w0:w0 + 16, n:2 * n], op=ALU.add
+                )
+                n = n // 2
+
+        def rest_sum(b, w0, nw, width):
+            h, c0 = b // 4, 32 * (b % 4) + w0
+            nc.vector.tensor_reduce(
+                out=num[h][:, c0:c0 + nw], in_=tb[b][:, w0:w0 + nw, 0:width], axis=AX.X, op=ALU.add
+            )
+
+        def final_a(h):
             rden = sm.tile([P, P], F32, name="rden")
             nc.vector.reciprocal(out=rden[:], in_=den[h][:])
             pooled = sm.tile([P, P], F32, name="pooled")
             nc.vector.tensor_tensor(out=pooled[:], in0=num[h][:], in1=rden[:], op=ALU.mult)
             pt = mp.tile([P, P], F32, name="pt", tag="misc")
             nc.tensor.transpose(pt[:], pooled[:], ident[:])
+            st[("pt", h)] = pt
+
+        def final_b(h):
+            pt = st[("pt", h)]
             o = sm.tile([P, P], F32, name="o")
             nc.vector.tensor_copy(out=o[:, 0:64], in_=pt[:, 0:64])
             xr = pt[:, 64:128].rearrange("w (j e) -> w j e", e=2)
@@ -293,31 +320,42 @@ def tile_deepseekv4csacompressor_t_kernel(tc, hidden_states, w_kv, w_gate, posit
             return 0 <= g < NG
 
         ctx.enter_context(tc.manual_schedule())
-        for k in range(-2, NG + 2):
-            if on(k + 2):
-                transposes(k + 2)
+        for k in range(-3, NG + 2):
+            if k < 0 and on(k + 1):
+                gate_mm(k + 1)
+            if on(k + 3):
+                transposes(k + 3)
             if on(k):
                 bias_add(k)
-            if on(k + 1):
-                quantise(k + 1)
-            if k == -1:
-                w_regroup(0)
-            if k == 0:
-                w_quantise(0)
+            if k >= 0 and on(k + 1):
+                gate_mm(k + 1)
+            if k >= 5 and k % 2 == 1:
+                rest_sum((k - 5) // 2, 0, 32, LEFT)
+            if k == NG + 1:
+                final_b(0)
+            if on(k - 2):
+                weigh(k - 2)
+            if on(k - 2) and k - 2 < NG - 1:
+                tree(k - 2)
+            if on(k - 1):
+                kv_mm(k - 1)
+            if k == NG:
+                final_a(0)
             if on(k + 2):
-                evac(k + 2)
+                quantise(k + 2)
+            if k == -2:
+                w_regroup(0)
+            if k == -1:
+                w_quantise(0)
+            if on(k + 3):
+                evac(k + 3)
+            if OFFLOAD and on(k - 1) and k - 1 < NG - 1:
+                kv_evac(k - 1)
+                weigh_late(k - 1)
             if on(k):
                 window_max(k)
-            if on(k + 1):
-                gate_mm(k + 1)
-            if on(k):
                 exps(k)
-            if on(k - 1):
-                weigh(k - 1)
-            if on(k):
-                kv_mm(k)
-            if on(k - 1):
-                pool_sum(k - 1)
-            if k == NG - 1:
-                final(0)
-        final(1)
+        rest_sum(7, 16, 16, 64)
+        rest_sum(7, 0, 16, LEFT)
+        final_a(1)
+        final_b(1)

@@ -18,7 +18,7 @@ FLOPS = 2 * 8192 * 512 * 512
 P = 128
 NG = 16
 NEG = -1.0e9
-OFFLOAD = False
+OFFLOAD = True
 LEFT = 8
 
 INV2PI = 0.15915493667125702

@@ -18,7 +18,7 @@ FLOPS = 2 * 8192 * 512 * 512
 P = 128
 NG = 16
 NEG = -1.0e9
-OFFLOAD = True
+PIN_FROM = 2
 LEFT = 8
 
 INV2PI = 0.15915493667125702
@@ -41,6 +41,7 @@ def tile_deepseekv4csacompressor_t_kernel(tc, hidden_states, w_kv, w_gate, posit
         xtp = ctx.enter_context(tc.psum_pool(name="xtp", bufs=2))
         gp = ctx.enter_context(tc.psum_pool(name="gp", bufs=2))
         kp = ctx.enter_context(tc.psum_pool(name="kp", bufs=1))
+        kxp = ctx.enter_context(tc.psum_pool(name="kxp", bufs=1))
         mp = ctx.enter_context(tc.psum_pool(name="mp", bufs=1))
 
         hid = hidden_states.rearrange("b s h -> (b s) h").rearrange("(g a p) h -> g p a h", a=4, p=P)
@@ -52,21 +53,26 @@ def tile_deepseekv4csacompressor_t_kernel(tc, hidden_states, w_kv, w_gate, posit
             x = xin.tile([P, 4, 512], BF16, name="x%d" % g)
             if g == 0:
                 nc.sync.dma_start(out=x[:, 0:2, :], in_=hid[g][:, 0:2, :])
+                load_w(1, w_gate)
                 nc.sync.dma_start(out=x[:, 2:4, :], in_=hid[g][:, 2:4, :])
             else:
                 nc.sync.dma_start(out=x[:], in_=hid[g])
             xs.append(x)
 
-        load_x(0)
         raws = []
         for nm in ("kv", "gate"):
             raws.append(const.tile([P, 4, 256], BF16, name="raw_%s" % nm))
-        for i, w in ((1, w_gate), (0, w_kv)):
+
+        def load_w(i, w):
             nc.sync.dma_start(
                 out=raws[i][:].rearrange("q (u e) n -> q u (e n)", u=2),
                 in_=w.rearrange("(u q e) n -> q u (e n)", u=2, e=2),
             )
-        for g in range(1, NG):
+
+        load_x(0)
+        load_x(1)
+        load_w(0, w_kv)
+        for g in range(2, NG):
             load_x(g)
 
         ident = const.tile([P, P], F32, name="ident")
@@ -179,7 +185,14 @@ def tile_deepseekv4csacompressor_t_kernel(tc, hidden_states, w_kv, w_gate, posit
         def quantise(g):
             codes = cpool.tile([P, 512], U32, name="codes", align_bytes=64)
             scl = cpool.tile([P, 512], U8, name="scl", align_bytes=64)
-            nc.vector.quantize_mx(out=codes[:].bitcast(FP8X4), scales=scl[:], in_=st[("grp", g)][:])
+            parts = 2 if g == 0 else 1
+            for i in range(parts):
+                n = 512 // parts
+                nc.vector.quantize_mx(
+                    out=codes[:, n * i:n * i + n].bitcast(FP8X4),
+                    scales=scl[:, n * i:n * i + n],
+                    in_=st[("grp", g)][:, 4 * n * i:4 * n * i + 4 * n],
+                )
             st[("q", g)] = (codes, scl)
 
         def mx(pool, nm, g, m, c0, c1):
@@ -197,19 +210,37 @@ def tile_deepseekv4csacompressor_t_kernel(tc, hidden_states, w_kv, w_gate, posit
             return ps
 
         def gate_mm(g):
+            if g == 0:
+                st[("g", g)] = (
+                    mx(gp, "gps", g, 2, 0, 256), mx(gp, "gps", g, 3, 0, 256),
+                    mx(kp, "klo", g, 2, 256, 512), mx(kp, "khi", g, 3, 256, 512),
+                )
+                return
             st[("g", g)] = (mx(gp, "gps", g, 2, 0, 512), mx(gp, "gps", g, 3, 0, 512))
 
         def kv_mm(g):
-            if OFFLOAD:
-                st[("kv", g)] = (
-                    mx(kp, "kla", g, 0, 0, 256), mx(kp, "khi", g, 1, 0, 512), mx(kp, "klb", g, 0, 256, 512)
-                )
-            else:
-                st[("kv", g)] = (mx(kp, "kla", g, 0, 0, 512), mx(kp, "khi", g, 1, 0, 512), None)
+            st[("kv", g)] = (mx(kp, "klo", g, 0, 0, 512), mx(kp, "khi", g, 1, 0, 512))
+            if g % 2 == 0:
+                st[("kx", g)] = mx(kxp, "kx", g, 0, 384, 512)
 
         def bias_add(g):
-            glo, ghi = st[("g", g)]
             t, w0 = tb[g // 2], 16 * (g % 2)
+            if g == 0:
+                for hf in range(2):
+                    nc.vector.tensor_tensor(
+                        out=t[:, 8 * hf + 1:8 * hf + 9, 0:32],
+                        in0=chunks(st[("g", g)][2 * hf][:]),
+                        in1=bias[:, 0:32].unsqueeze(1).to_broadcast([P, 8, 32]),
+                        op=ALU.add,
+                    )
+                    nc.vector.tensor_tensor(
+                        out=t[:, 8 * hf:8 * hf + 8, 32:64],
+                        in0=chunks(st[("g", g)][2 * hf + 1][:]),
+                        in1=bias[:, 32:64].unsqueeze(1).to_broadcast([P, 8, 32]),
+                        op=ALU.add,
+                    )
+                return
+            glo, ghi = st[("g", g)]
             n = 16 - g % 2
             nc.vector.tensor_tensor(
                 out=t[:, w0 + 1:w0 + 1 + n, 0:32],
@@ -244,38 +275,22 @@ def tile_deepseekv4csacompressor_t_kernel(tc, hidden_states, w_kv, w_gate, posit
                     accum_out=den[h][:, c0 + w:c0 + w + 1],
                 )
 
-        def kv_evac(g):
-            kvb = sm.tile([P, 256], F32, name="kvb", bufs=3)
-            nc.scalar.copy(out=kvb[:], in_=st[("kv", g)][2][:])
-            st[("kvb", g)] = kvb
+        def kvs_copy(g):
+            kvs = sm.tile([P, 32], F32, name="kvs")
+            nc.scalar.copy(out=kvs[:], in_=st[("kx", g)][:, 96:128])
+            st[("kvs", g)] = kvs
 
         def mul(eng, view, other):
             eng.tensor_tensor(out=view, in0=view, in1=other, op=ALU.mult)
 
         def weigh(g):
-            kla, khi, klb = st[("kv", g)]
+            klo, khi = st[("kv", g)]
             t, w0 = tb[g // 2], 16 * (g % 2)
-            if not OFFLOAD:
-                mul(nc.vector, t[:, w0 + 1:w0 + 16, 0:32], chunks(kla[:, 0:480]))
-                if g % 2 == 0:
-                    kvs = sm.tile([P, 32], F32, name="kvs")
-                    nc.vector.tensor_copy(out=kvs[:], in_=kla[:, 480:512])
-                    st[("kvs", g)] = kvs
-                else:
-                    mul(nc.vector, t[:, w0, 0:32], st[("kvs", g - 1)][:])
-                mul(nc.vector, t[:, w0:w0 + 16, 32:64], chunks(khi[:]))
-                return
-            mul(nc.vector, t[:, w0 + 1:w0 + 9, 0:32], chunks(kla[:]))
+            mul(nc.vector, t[:, w0 + 1:w0 + 16, 0:32], chunks(klo[:, 0:480]))
             mul(nc.vector, t[:, w0:w0 + 16, 32:64], chunks(khi[:]))
-            if g == NG - 1:
-                mul(nc.vector, t[:, w0 + 9:w0 + 16, 0:32], chunks(klb[:, 0:224]))
-                mul(nc.vector, t[:, w0, 0:32], st[("kvb", g - 1)][:, 224:256])
 
-        def weigh_late(g):
-            t, w0 = tb[g // 2], 16 * (g % 2)
-            mul(nc.gpsimd, t[:, w0 + 9:w0 + 16, 0:32], chunks(st[("kvb", g)][:, 0:224]))
-            if g % 2 == 1:
-                mul(nc.gpsimd, t[:, w0, 0:32], st[("kvb", g - 1)][:, 224:256])
+        def weigh_first(eng, g):
+            mul(eng, tb[g // 2][:, 16, 0:32], st[("kvs", g - 1)][:])
 
         def tree(g):
             t, w0 = tb[g // 2], 16 * (g % 2)
@@ -292,12 +307,12 @@ def tile_deepseekv4csacompressor_t_kernel(tc, hidden_states, w_kv, w_gate, posit
                 out=num[h][:, c0:c0 + nw], in_=tb[b][:, w0:w0 + nw, 0:width], axis=AX.X, op=ALU.add
             )
 
-        def final_a(h):
+        def final_a(h, pool):
             rden = sm.tile([P, P], F32, name="rden")
             nc.vector.reciprocal(out=rden[:], in_=den[h][:])
             pooled = sm.tile([P, P], F32, name="pooled")
             nc.vector.tensor_tensor(out=pooled[:], in0=num[h][:], in1=rden[:], op=ALU.mult)
-            pt = mp.tile([P, P], F32, name="pt", tag="misc")
+            pt = pool.tile([P, P], F32, name="pt", tag="misc" if h == 0 else "kx")
             nc.tensor.transpose(pt[:], pooled[:], ident[:])
             st[("pt", h)] = pt
 
@@ -319,43 +334,51 @@ def tile_deepseekv4csacompressor_t_kernel(tc, hidden_states, w_kv, w_gate, posit
         def on(g):
             return 0 <= g < NG
 
-        ctx.enter_context(tc.manual_schedule())
-        for k in range(-3, NG + 2):
-            if k < 0 and on(k + 1):
-                gate_mm(k + 1)
+        transposes(0)
+        evac(0)
+        quantise(0)
+        gate_mm(0)
+        transposes(1)
+        evac(1)
+        quantise(1)
+        w_regroup(0)
+        transposes(2)
+        evac(2)
+        w_quantise(0)
+        for k in range(0, NG + 2):
+            if k == PIN_FROM:
+                ctx.enter_context(tc.manual_schedule())
             if on(k + 3):
                 transposes(k + 3)
             if on(k):
                 bias_add(k)
-            if k >= 0 and on(k + 1):
+            if on(k + 1):
                 gate_mm(k + 1)
             if k >= 5 and k % 2 == 1:
                 rest_sum((k - 5) // 2, 0, 32, LEFT)
-            if k == NG + 1:
-                final_b(0)
             if on(k - 2):
                 weigh(k - 2)
+            if k - 2 == NG - 1:
+                weigh_first(nc.vector, k - 2)
             if on(k - 2) and k - 2 < NG - 1:
                 tree(k - 2)
+            if on(k - 1) and (k - 1) % 2 == 1 and k - 1 < NG - 1:
+                weigh_first(nc.gpsimd, k - 1)
             if on(k - 1):
                 kv_mm(k - 1)
             if k == NG:
-                final_a(0)
+                final_a(0, mp)
             if on(k + 2):
                 quantise(k + 2)
-            if k == -2:
-                w_regroup(0)
-            if k == -1:
-                w_quantise(0)
             if on(k + 3):
                 evac(k + 3)
-            if OFFLOAD and on(k - 1) and k - 1 < NG - 1:
-                kv_evac(k - 1)
-                weigh_late(k - 1)
+            if on(k - 1) and (k - 1) % 2 == 0:
+                kvs_copy(k - 1)
             if on(k):
                 window_max(k)
                 exps(k)
         rest_sum(7, 16, 16, 64)
         rest_sum(7, 0, 16, LEFT)
-        final_a(1)
+        final_a(1, kxp)
+        final_b(0)
         final_b(1)

@@ -18,8 +18,8 @@ FLOPS = 2 * 8192 * 512 * 512
 P = 128
 NG = 16
 NEG = -1.0e9
-PIN_FROM = 2
-LEFT = 8
+OFFLOAD = True
+LEFT = 16
 
 INV2PI = 0.15915493667125702
 TWO_PI_1 = 6.28125
@@ -41,7 +41,6 @@ def tile_deepseekv4csacompressor_t_kernel(tc, hidden_states, w_kv, w_gate, posit
         xtp = ctx.enter_context(tc.psum_pool(name="xtp", bufs=2))
         gp = ctx.enter_context(tc.psum_pool(name="gp", bufs=2))
         kp = ctx.enter_context(tc.psum_pool(name="kp", bufs=1))
-        kxp = ctx.enter_context(tc.psum_pool(name="kxp", bufs=1))
         mp = ctx.enter_context(tc.psum_pool(name="mp", bufs=1))
 
         hid = hidden_states.rearrange("b s h -> (b s) h").rearrange("(g a p) h -> g p a h", a=4, p=P)
@@ -53,26 +52,21 @@ def tile_deepseekv4csacompressor_t_kernel(tc, hidden_states, w_kv, w_gate, posit
             x = xin.tile([P, 4, 512], BF16, name="x%d" % g)
             if g == 0:
                 nc.sync.dma_start(out=x[:, 0:2, :], in_=hid[g][:, 0:2, :])
-                load_w(1, w_gate)
                 nc.sync.dma_start(out=x[:, 2:4, :], in_=hid[g][:, 2:4, :])
             else:
                 nc.sync.dma_start(out=x[:], in_=hid[g])
             xs.append(x)
 
+        load_x(0)
         raws = []
         for nm in ("kv", "gate"):
             raws.append(const.tile([P, 4, 256], BF16, name="raw_%s" % nm))
-
-        def load_w(i, w):
+        for i, w in ((1, w_gate), (0, w_kv)):
             nc.sync.dma_start(
                 out=raws[i][:].rearrange("q (u e) n -> q u (e n)", u=2),
                 in_=w.rearrange("(u q e) n -> q u (e n)", u=2, e=2),
             )
-
-        load_x(0)
-        load_x(1)
-        load_w(0, w_kv)
-        for g in range(2, NG):
+        for g in range(1, NG):
             load_x(g)
 
         ident = const.tile([P, P], F32, name="ident")
@@ -185,14 +179,7 @@ def tile_deepseekv4csacompressor_t_kernel(tc, hidden_states, w_kv, w_gate, posit
         def quantise(g):
             codes = cpool.tile([P, 512], U32, name="codes", align_bytes=64)
             scl = cpool.tile([P, 512], U8, name="scl", align_bytes=64)
-            parts = 2 if g == 0 else 1
-            for i in range(parts):
-                n = 512 // parts
-                nc.vector.quantize_mx(
-                    out=codes[:, n * i:n * i + n].bitcast(FP8X4),
-                    scales=scl[:, n * i:n * i + n],
-                    in_=st[("grp", g)][:, 4 * n * i:4 * n * i + 4 * n],
-                )
+            nc.vector.quantize_mx(out=codes[:].bitcast(FP8X4), scales=scl[:], in_=st[("grp", g)][:])
             st[("q", g)] = (codes, scl)
 
         def mx(pool, nm, g, m, c0, c1):
@@ -210,37 +197,19 @@ def tile_deepseekv4csacompressor_t_kernel(tc, hidden_states, w_kv, w_gate, posit
             return ps
 
         def gate_mm(g):
-            if g == 0:
-                st[("g", g)] = (
-                    mx(gp, "gps", g, 2, 0, 256), mx(gp, "gps", g, 3, 0, 256),
-                    mx(kp, "klo", g, 2, 256, 512), mx(kp, "khi", g, 3, 256, 512),
-                )
-                return
             st[("g", g)] = (mx(gp, "gps", g, 2, 0, 512), mx(gp, "gps", g, 3, 0, 512))
 
         def kv_mm(g):
-            st[("kv", g)] = (mx(kp, "klo", g, 0, 0, 512), mx(kp, "khi", g, 1, 0, 512))
-            if g % 2 == 0:
-                st[("kx", g)] = mx(kxp, "kx", g, 0, 384, 512)
+            if OFFLOAD:
+                st[("kv", g)] = (
+                    mx(kp, "kla", g, 0, 0, 256), mx(kp, "khi", g, 1, 0, 512), mx(kp, "klb", g, 0, 256, 512)
+                )
+            else:
+                st[("kv", g)] = (mx(kp, "kla", g, 0, 0, 512), mx(kp, "khi", g, 1, 0, 512), None)
 
         def bias_add(g):
-            t, w0 = tb[g // 2], 16 * (g % 2)
-            if g == 0:
-                for hf in range(2):
-                    nc.vector.tensor_tensor(
-                        out=t[:, 8 * hf + 1:8 * hf + 9, 0:32],
-                        in0=chunks(st[("g", g)][2 * hf][:]),
-                        in1=bias[:, 0:32].unsqueeze(1).to_broadcast([P, 8, 32]),
-                        op=ALU.add,
-                    )
-                    nc.vector.tensor_tensor(
-                        out=t[:, 8 * hf:8 * hf + 8, 32:64],
-                        in0=chunks(st[("g", g)][2 * hf + 1][:]),
-                        in1=bias[:, 32:64].unsqueeze(1).to_broadcast([P, 8, 32]),
-                        op=ALU.add,
-                    )
-                return
             glo, ghi = st[("g", g)]
+            t, w0 = tb[g // 2], 16 * (g % 2)
             n = 16 - g % 2
             nc.vector.tensor_tensor(
                 out=t[:, w0 + 1:w0 + 1 + n, 0:32],
@@ -275,22 +244,38 @@ def tile_deepseekv4csacompressor_t_kernel(tc, hidden_states, w_kv, w_gate, posit
                     accum_out=den[h][:, c0 + w:c0 + w + 1],
                 )
 
-        def kvs_copy(g):
-            kvs = sm.tile([P, 32], F32, name="kvs")
-            nc.scalar.copy(out=kvs[:], in_=st[("kx", g)][:, 96:128])
-            st[("kvs", g)] = kvs
+        def kv_evac(g):
+            kvb = sm.tile([P, 256], F32, name="kvb", bufs=3)
+            nc.scalar.copy(out=kvb[:], in_=st[("kv", g)][2][:])
+            st[("kvb", g)] = kvb
 
         def mul(eng, view, other):
             eng.tensor_tensor(out=view, in0=view, in1=other, op=ALU.mult)
 
         def weigh(g):
-            klo, khi = st[("kv", g)]
+            kla, khi, klb = st[("kv", g)]
             t, w0 = tb[g // 2], 16 * (g % 2)
-            mul(nc.vector, t[:, w0 + 1:w0 + 16, 0:32], chunks(klo[:, 0:480]))
+            if not OFFLOAD:
+                mul(nc.vector, t[:, w0 + 1:w0 + 16, 0:32], chunks(kla[:, 0:480]))
+                if g % 2 == 0:
+                    kvs = sm.tile([P, 32], F32, name="kvs")
+                    nc.vector.tensor_copy(out=kvs[:], in_=kla[:, 480:512])
+                    st[("kvs", g)] = kvs
+                else:
+                    mul(nc.vector, t[:, w0, 0:32], st[("kvs", g - 1)][:])
+                mul(nc.vector, t[:, w0:w0 + 16, 32:64], chunks(khi[:]))
+                return
+            mul(nc.vector, t[:, w0 + 1:w0 + 9, 0:32], chunks(kla[:]))
             mul(nc.vector, t[:, w0:w0 + 16, 32:64], chunks(khi[:]))
+            if g == NG - 1:
+                mul(nc.vector, t[:, w0 + 9:w0 + 16, 0:32], chunks(klb[:, 0:224]))
+                mul(nc.vector, t[:, w0, 0:32], st[("kvb", g - 1)][:, 224:256])
 
-        def weigh_first(eng, g):
-            mul(eng, tb[g // 2][:, 16, 0:32], st[("kvs", g - 1)][:])
+        def weigh_late(g):
+            t, w0 = tb[g // 2], 16 * (g % 2)
+            mul(nc.gpsimd, t[:, w0 + 9:w0 + 16, 0:32], chunks(st[("kvb", g)][:, 0:224]))
+            if g % 2 == 1:
+                mul(nc.gpsimd, t[:, w0, 0:32], st[("kvb", g - 1)][:, 224:256])
 
         def tree(g):
             t, w0 = tb[g // 2], 16 * (g % 2)
@@ -307,12 +292,12 @@ def tile_deepseekv4csacompressor_t_kernel(tc, hidden_states, w_kv, w_gate, posit
                 out=num[h][:, c0:c0 + nw], in_=tb[b][:, w0:w0 + nw, 0:width], axis=AX.X, op=ALU.add
             )
 
-        def final_a(h, pool):
+        def final_a(h):
             rden = sm.tile([P, P], F32, name="rden")
             nc.vector.reciprocal(out=rden[:], in_=den[h][:])
             pooled = sm.tile([P, P], F32, name="pooled")
             nc.vector.tensor_tensor(out=pooled[:], in0=num[h][:], in1=rden[:], op=ALU.mult)
-            pt = pool.tile([P, P], F32, name="pt", tag="misc" if h == 0 else "kx")
+            pt = mp.tile([P, P], F32, name="pt", tag="misc")
             nc.tensor.transpose(pt[:], pooled[:], ident[:])
             st[("pt", h)] = pt
 
@@ -334,51 +319,43 @@ def tile_deepseekv4csacompressor_t_kernel(tc, hidden_states, w_kv, w_gate, posit
         def on(g):
             return 0 <= g < NG
 
-        transposes(0)
-        evac(0)
-        quantise(0)
-        gate_mm(0)
-        transposes(1)
-        evac(1)
-        quantise(1)
-        w_regroup(0)
-        transposes(2)
-        evac(2)
-        w_quantise(0)
-        for k in range(0, NG + 2):
-            if k == PIN_FROM:
-                ctx.enter_context(tc.manual_schedule())
+        ctx.enter_context(tc.manual_schedule())
+        for k in range(-3, NG + 2):
+            if k < 0 and on(k + 1):
+                gate_mm(k + 1)
             if on(k + 3):
                 transposes(k + 3)
             if on(k):
                 bias_add(k)
-            if on(k + 1):
+            if k >= 0 and on(k + 1):
                 gate_mm(k + 1)
             if k >= 5 and k % 2 == 1:
                 rest_sum((k - 5) // 2, 0, 32, LEFT)
+            if k == NG + 1:
+                final_b(0)
             if on(k - 2):
                 weigh(k - 2)
-            if k - 2 == NG - 1:
-                weigh_first(nc.vector, k - 2)
             if on(k - 2) and k - 2 < NG - 1:
                 tree(k - 2)
-            if on(k - 1) and (k - 1) % 2 == 1 and k - 1 < NG - 1:
-                weigh_first(nc.gpsimd, k - 1)
             if on(k - 1):
                 kv_mm(k - 1)
             if k == NG:
-                final_a(0, mp)
+                final_a(0)
             if on(k + 2):
                 quantise(k + 2)
+            if k == -2:
+                w_regroup(0)
+            if k == -1:
+                w_quantise(0)
             if on(k + 3):
                 evac(k + 3)
-            if on(k - 1) and (k - 1) % 2 == 0:
-                kvs_copy(k - 1)
+            if OFFLOAD and on(k - 1) and k - 1 < NG - 1:
+                kv_evac(k - 1)
+                weigh_late(k - 1)
             if on(k):
                 window_max(k)
                 exps(k)
         rest_sum(7, 16, 16, 64)
         rest_sum(7, 0, 16, LEFT)
-        final_a(1, kxp)
-        final_b(0)
+        final_a(1)
         final_b(1)

@@ -57,16 +57,21 @@ def tile_deepseekv4csacompressor_t_kernel(tc, hidden_states, w_kv, w_gate, posit
                 nc.sync.dma_start(out=x[:], in_=hid[g])
             xs.append(x)
 
-        load_x(0)
         raws = []
         for nm in ("kv", "gate"):
             raws.append(const.tile([P, 4, 256], BF16, name="raw_%s" % nm))
-        for i, w in ((1, w_gate), (0, w_kv)):
+
+        def load_w(i, w):
             nc.sync.dma_start(
                 out=raws[i][:].rearrange("q (u e) n -> q u (e n)", u=2),
                 in_=w.rearrange("(u q e) n -> q u (e n)", u=2, e=2),
             )
-        for g in range(1, NG):
+
+        load_x(0)
+        load_w(1, w_gate)
+        load_x(1)
+        load_w(0, w_kv)
+        for g in range(2, NG):
             load_x(g)
 
         ident = const.tile([P, P], F32, name="ident")
@@ -99,31 +104,47 @@ def tile_deepseekv4csacompressor_t_kernel(tc, hidden_states, w_kv, w_gate, posit
         nc.vector.tensor_copy(out=posf[:], in_=posi[:])
         ang = small("ang")
         for j in range(32):
-            nc.vector.tensor_scalar(
-                out=ang[:, j:j + 1], in0=posf[:, 0:1], scalar1=10000.0 ** (-j / 32.0), scalar2=None, op0=ALU.mult
+            nc.gpsimd.tensor_scalar(
+                out=ang[:, j:j + 1], in0=posf[:, 0:1], scalar1=10000.0 ** (-j / 32.0), scalar2=0.0,
+                op0=ALU.mult, op1=ALU.add,
             )
         xk = small("xk")
-        nc.vector.tensor_scalar(out=xk[:], in0=ang[:], scalar1=INV2PI, scalar2=None, op0=ALU.mult)
+        nc.gpsimd.tensor_scalar(out=xk[:], in0=ang[:], scalar1=INV2PI, scalar2=0.0, op0=ALU.mult, op1=ALU.add)
         kc = small("kc", I32)
-        nc.vector.tensor_copy(out=kc[:], in_=xk[:])
+        nc.gpsimd.tensor_copy(out=kc[:], in_=xk[:])
         ki = small("ki", I32)
-        nc.vector.tensor_single_scalar(out=ki[:], in_=kc[:], scalar=255, op=ALU.bitwise_and)
         kf = small("kf")
-        nc.vector.tensor_copy(out=kf[:], in_=ki[:])
-        r_prev = ang
-        for n, c in enumerate((TWO_PI_1, TWO_PI_2, TWO_PI_3)):
-            r = small("r%d" % n)
-            nc.vector.scalar_tensor_tensor(out=r[:], in0=kf[:], scalar=-c, in1=r_prev[:], op0=ALU.mult, op1=ALU.add)
-            r_prev = r
-        ab = small("ab")
-        nc.vector.scalar_tensor_tensor(out=ab[:], in0=r_prev[:], scalar=-1.0, in1=r_prev[:], op0=ALU.mult, op1=ALU.max)
-        uu = small("uu")
-        nc.vector.tensor_scalar(out=uu[:], in0=ab[:], scalar1=-HALF_PI_1, scalar2=-HALF_PI_2, op0=ALU.add, op1=ALU.add)
+        red = small("red")
         ss = const.tile([P, 32, 2], F32, name="ss")
         cosT = small("cosT")
-        nc.scalar.activation(out=ss[:, :, 1], in_=r_prev[:], func=ACT.Sin)
-        nc.scalar.activation(out=ss[:, :, 0], in_=r_prev[:], func=ACT.Sin, scale=-1.0)
-        nc.scalar.activation(out=cosT[:], in_=uu[:], func=ACT.Sin, scale=-1.0)
+        sq = small("sq")
+        warm = small("warm", F32, 1)
+        nc.scalar.activation(out=warm[:], in_=posf[:], func=ACT.Exp, scale=0.0)
+
+        def turns_a():
+            nc.vector.tensor_single_scalar(out=ki[:], in_=kc[:], scalar=255, op=ALU.bitwise_and)
+
+        def turns_b():
+            nc.vector.tensor_copy(out=kf[:], in_=ki[:])
+
+        def reduce_angle():
+            r_prev = ang
+            for n, c in enumerate((TWO_PI_1, TWO_PI_2, TWO_PI_3)):
+                step = small("step%d" % n)
+                nc.gpsimd.tensor_scalar(out=step[:], in0=kf[:], scalar1=-c, scalar2=0.0, op0=ALU.mult, op1=ALU.add)
+                r = red if n == 2 else small("r%d" % n)
+                nc.gpsimd.tensor_tensor(out=r[:], in0=step[:], in1=r_prev[:], op=ALU.add)
+                r_prev = r
+
+        def sin_cos():
+            nc.scalar.activation(out=ss[:, :, 1], in_=red[:], func=ACT.Sin)
+            nc.scalar.activation(out=ss[:, :, 0], in_=red[:], func=ACT.Sin, scale=-1.0)
+            half = small("half")
+            nc.scalar.activation(out=half[:], in_=red[:], func=ACT.Sin, scale=0.5)
+            nc.scalar.activation(out=sq[:], in_=half[:], func=ACT.Square)
+
+        def cos_finish():
+            nc.gpsimd.tensor_scalar(out=cosT[:], in0=sq[:], scalar1=-2.0, scalar2=1.0, op0=ALU.mult, op1=ALU.add)
 
         wgrp = const.tile([P, 512, 4], BF16, name="wgrp", align_bytes=64)
         wcodes = const.tile([P, 512], U32, name="wcodes", align_bytes=64)
@@ -297,7 +318,10 @@ def tile_deepseekv4csacompressor_t_kernel(tc, hidden_states, w_kv, w_gate, posit
             nc.vector.reciprocal(out=rden[:], in_=den[h][:])
             pooled = sm.tile([P, P], F32, name="pooled")
             nc.vector.tensor_tensor(out=pooled[:], in0=num[h][:], in1=rden[:], op=ALU.mult)
-            pt = mp.tile([P, P], F32, name="pt", tag="misc")
+            if h == 0:
+                pt = mp.tile([P, P], F32, name="pt", tag="misc")
+            else:
+                pt = kp.tile([P, P], F32, name="pt", tag="klb")
             nc.tensor.transpose(pt[:], pooled[:], ident[:])
             st[("pt", h)] = pt
 
@@ -320,19 +344,47 @@ def tile_deepseekv4csacompressor_t_kernel(tc, hidden_states, w_kv, w_gate, posit
             return 0 <= g < NG
 
         ctx.enter_context(tc.manual_schedule())
-        for k in range(-3, NG + 2):
-            if k < 0 and on(k + 1):
-                gate_mm(k + 1)
+        transposes(0)
+        evac(0)
+        transposes(1)
+        evac(1)
+        quantise(0)
+        w_regroup(0)
+        gate_mm(0)
+        transposes(2)
+        evac(2)
+        bias_add(0)
+        quantise(1)
+        gate_mm(1)
+        transposes(3)
+        evac(3)
+        window_max(0)
+        exps(0)
+        transposes(4)
+        bias_add(1)
+        quantise(2)
+        gate_mm(2)
+        w_quantise(0)
+        kv_mm(0)
+        quantise(3)
+        evac(4)
+        kv_evac(0)
+        weigh_late(0)
+        window_max(1)
+        exps(1)
+        for k in range(2, NG + 2):
             if on(k + 3):
                 transposes(k + 3)
             if on(k):
                 bias_add(k)
-            if k >= 0 and on(k + 1):
+            if k == 3:
+                turns_a()
+            if k == 4:
+                turns_b()
+            if on(k + 1):
                 gate_mm(k + 1)
             if k >= 5 and k % 2 == 1:
                 rest_sum((k - 5) // 2, 0, 32, LEFT)
-            if k == NG + 1:
-                final_b(0)
             if on(k - 2):
                 weigh(k - 2)
             if on(k - 2) and k - 2 < NG - 1:
@@ -343,19 +395,21 @@ def tile_deepseekv4csacompressor_t_kernel(tc, hidden_states, w_kv, w_gate, posit
                 final_a(0)
             if on(k + 2):
                 quantise(k + 2)
-            if k == -2:
-                w_regroup(0)
-            if k == -1:
-                w_quantise(0)
             if on(k + 3):
                 evac(k + 3)
             if OFFLOAD and on(k - 1) and k - 1 < NG - 1:
                 kv_evac(k - 1)
                 weigh_late(k - 1)
+            if k == 5:
+                reduce_angle()
             if on(k):
                 window_max(k)
                 exps(k)
+            if k == NG - 1:
+                sin_cos()
+        cos_finish()
         rest_sum(7, 16, 16, 64)
         rest_sum(7, 0, 16, LEFT)
         final_a(1)
+        final_b(0)
         final_b(1)

from contextlib import ExitStack

import concourse.mybir as mybir
from concourse.masks import make_identity

F32 = mybir.dt.float32
BF16 = mybir.dt.bfloat16
I32 = mybir.dt.int32
U32 = mybir.dt.uint32
U8 = mybir.dt.uint8
FP8X4 = mybir.dt.float8_e4m3fn_x4
ALU = mybir.AluOpType
ACT = mybir.ActivationFunctionType
AX = mybir.AxisListType

FLOPS = 2 * 8192 * 512 * 512

P = 128
NG = 16
NEG = -1.0e9
OFFLOAD = True
LEFT = 16

INV2PI = 0.15915493667125702
TWO_PI_1 = 6.28125
TWO_PI_2 = 0.0019352436065673828
TWO_PI_3 = 6.357301884918343e-08
HALF_PI_1 = 1.5707963705062866
HALF_PI_2 = -4.371138828673793e-08


def tile_deepseekv4csacompressor_t_kernel(tc, hidden_states, w_kv, w_gate, position_bias, out):
    nc = tc.nc
    with ExitStack() as ctx:
        const = ctx.enter_context(tc.tile_pool(name="const", bufs=1))
        xin = ctx.enter_context(tc.tile_pool(name="xin", bufs=1))
        twp = ctx.enter_context(tc.tile_pool(name="twp", bufs=1))
        gpool = ctx.enter_context(tc.tile_pool(name="gpool", bufs=3))
        cpool = ctx.enter_context(tc.tile_pool(name="cpool", bufs=4))
        sm = ctx.enter_context(tc.tile_pool(name="sm", bufs=2))
        xtp = ctx.enter_context(tc.psum_pool(name="xtp", bufs=2))
        gp = ctx.enter_context(tc.psum_pool(name="gp", bufs=2))
        kp = ctx.enter_context(tc.psum_pool(name="kp", bufs=1))
        mp = ctx.enter_context(tc.psum_pool(name="mp", bufs=1))

        hid = hidden_states.rearrange("b s h -> (b s) h").rearrange("(g a p) h -> g p a h", a=4, p=P)
        outr = out.rearrange("b i c -> (b i) c")

        xs = []

        def load_x(g):
            x = xin.tile([P, 4, 512], BF16, name="x%d" % g)
            if g == 0:
                nc.sync.dma_start(out=x[:, 0:2, :], in_=hid[g][:, 0:2, :])
                nc.sync.dma_start(out=x[:, 2:4, :], in_=hid[g][:, 2:4, :])
            else:
                nc.sync.dma_start(out=x[:], in_=hid[g])
            xs.append(x)

        raws = []
        for nm in ("kv", "gate"):
            raws.append(const.tile([P, 4, 256], BF16, name="raw_%s" % nm))

        def load_w(i, w):
            nc.sync.dma_start(
                out=raws[i][:].rearrange("q (u e) n -> q u (e n)", u=2),
                in_=w.rearrange("(u q e) n -> q u (e n)", u=2, e=2),
            )

        load_x(0)
        load_w(1, w_gate)
        load_x(1)
        load_w(0, w_kv)
        for g in range(2, NG):
            load_x(g)

        ident = const.tile([P, P], F32, name="ident")
        make_identity(nc, ident[:])

        bz = const.tile([P, P], BF16, name="bz")
        nc.vector.memset(bz[64:128, :], 0.0)
        nc.scalar.dma_start(out=bz[0:64, :], in_=position_bias)

        tb = []
        for b in range(NG // 2):
            tb.append(twp.tile([P, 32, 64], F32, name="tb%d" % b))
            nc.gpsimd.memset(tb[b][:, 0, 0:32], NEG)
        den = []
        num = []
        for h in range(2):
            den.append(const.tile([P, P], F32, name="den%d" % h))
            num.append(const.tile([P, P], F32, name="num%d" % h))

        def small(nm, dt=F32, w=32):
            return const.tile([P, w], dt, name=nm)

        pidx = small("pidx", I32, 1)
        nc.gpsimd.iota(pidx[:], pattern=[[0, 1]], base=0, channel_multiplier=1)
        posi = small("posi", I32, 1)
        nc.vector.tensor_scalar(
            out=posi[:], in0=pidx[:], scalar1=31, scalar2=5, op0=ALU.bitwise_and, op1=ALU.logical_shift_left
        )
        posf = small("posf", F32, 1)
        nc.vector.tensor_copy(out=posf[:], in_=posi[:])
        ang = small("ang")
        for j in range(32):
            nc.gpsimd.tensor_scalar(
                out=ang[:, j:j + 1], in0=posf[:, 0:1], scalar1=10000.0 ** (-j / 32.0), scalar2=0.0,
                op0=ALU.mult, op1=ALU.add,
            )
        xk = small("xk")
        nc.gpsimd.tensor_scalar(out=xk[:], in0=ang[:], scalar1=INV2PI, scalar2=0.0, op0=ALU.mult, op1=ALU.add)
        kc = small("kc", I32)
        nc.gpsimd.tensor_copy(out=kc[:], in_=xk[:])
        ki = small("ki", I32)
        kf = small("kf")
        red = small("red")
        ss = const.tile([P, 32, 2], F32, name="ss")
        cosT = small("cosT")
        sq = small("sq")
        warm = small("warm", F32, 1)
        nc.scalar.activation(out=warm[:], in_=posf[:], func=ACT.Exp, scale=0.0)

        def turns_a():
            nc.vector.tensor_single_scalar(out=ki[:], in_=kc[:], scalar=255, op=ALU.bitwise_and)

        def turns_b():
            nc.vector.tensor_copy(out=kf[:], in_=ki[:])

        def reduce_angle():
            r_prev = ang
            for n, c in enumerate((TWO_PI_1, TWO_PI_2, TWO_PI_3)):
                step = small("step%d" % n)
                nc.gpsimd.tensor_scalar(out=step[:], in0=kf[:], scalar1=-c, scalar2=0.0, op0=ALU.mult, op1=ALU.add)
                r = red if n == 2 else small("r%d" % n)
                nc.gpsimd.tensor_tensor(out=r[:], in0=step[:], in1=r_prev[:], op=ALU.add)
                r_prev = r

        def sin_cos():
            nc.scalar.activation(out=ss[:, :, 1], in_=red[:], func=ACT.Sin)
            nc.scalar.activation(out=ss[:, :, 0], in_=red[:], func=ACT.Sin, scale=-1.0)
            half = small("half")
            nc.scalar.activation(out=half[:], in_=red[:], func=ACT.Sin, scale=0.5)
            nc.scalar.activation(out=sq[:], in_=half[:], func=ACT.Square)

        def cos_finish():
            nc.gpsimd.tensor_scalar(out=cosT[:], in0=sq[:], scalar1=-2.0, scalar2=1.0, op0=ALU.mult, op1=ALU.add)

        wgrp = const.tile([P, 512, 4], BF16, name="wgrp", align_bytes=64)
        wcodes = const.tile([P, 512], U32, name="wcodes", align_bytes=64)
        wscl = const.tile([P, 512], U8, name="wscl", align_bytes=64)

        def w_regroup(i):
            cols = slice(256 * i, 256 * i + 256)
            nc.vector.tensor_copy(out=wgrp[:, cols, :], in_=raws[i][:].rearrange("q t n -> q n t"))

        def w_quantise(i):
            cols = slice(256 * i, 256 * i + 256)
            nc.vector.quantize_mx(
                out=wcodes[:, cols].bitcast(FP8X4),
                scales=wscl[:, cols],
                in_=wgrp[:, cols, :].rearrange("q n t -> q (n t)"),
            )

        bzf = const.tile([P, P], F32, name="bzf")
        nc.vector.tensor_copy(out=bzf[:], in_=bz[:])
        bT = mp.tile([P, P], F32, name="bT", tag="misc")
        nc.tensor.transpose(bT[:], bzf[:], ident[:])
        w_regroup(1)
        bias = const.tile([P, 64], F32, name="bias")
        nc.vector.tensor_copy(out=bias[:], in_=bT[:, 0:64])
        w_quantise(1)

        st = {}

        def chunks(ap):
            return ap.rearrange("c (j s) -> c j s", s=32)

        def transposes(g):
            xw = xs[g][:].bitcast(F32)
            tiles = []
            for hf in range(2):
                xt = xtp.tile([P, 2, 2, P], F32, name="xt")
                for a in range(2):
                    for u in range(2):
                        nc.tensor.transpose(xt[:, a, u, :], xw[:, 2 * hf + a, 128 * u:128 * u + 128], ident[:])
                tiles.append(xt)
            st[("xt", g)] = tiles

        def evac(g):
            grp = gpool.tile([P, 2048], BF16, name="grp", align_bytes=64)
            gw = grp[:].bitcast(F32).rearrange("q (a p u) -> q a p u", a=4, u=2)
            for hf in range(2):
                nc.scalar.copy(
                    out=gw[:, 2 * hf:2 * hf + 2, :, :],
                    in_=st[("xt", g)][hf][:].rearrange("q a u p -> q a p u"),
                )
            st[("grp", g)] = grp

        def quantise(g):
            codes = cpool.tile([P, 512], U32, name="codes", align_bytes=64)
            scl = cpool.tile([P, 512], U8, name="scl", align_bytes=64)
            nc.vector.quantize_mx(out=codes[:].bitcast(FP8X4), scales=scl[:], in_=st[("grp", g)][:])
            st[("q", g)] = (codes, scl)

        def mx(pool, nm, g, m, c0, c1):
            codes, scl = st[("q", g)]
            ps = pool.tile([P, c1 - c0], F32, name=nm)
            nc.tensor.matmul_mx(
                out=ps[:],
                lhsT=wcodes[:, 128 * m:128 * m + 128].bitcast(FP8X4),
                lhsT_scale=wscl[:, 128 * m:128 * m + 128],
                rhs=codes[:, c0:c1].bitcast(FP8X4),
                rhs_scale=scl[:, c0:c1],
                start=True,
                stop=True,
            )
            return ps

        def gate_mm(g):
            st[("g", g)] = (mx(gp, "gps", g, 2, 0, 512), mx(gp, "gps", g, 3, 0, 512))

        def kv_mm(g):
            if OFFLOAD:
                st[("kv", g)] = (
                    mx(kp, "kla", g, 0, 0, 256), mx(kp, "khi", g, 1, 0, 512), mx(kp, "klb", g, 0, 256, 512)
                )
            else:
                st[("kv", g)] = (mx(kp, "kla", g, 0, 0, 512), mx(kp, "khi", g, 1, 0, 512), None)

        def bias_add(g):
            glo, ghi = st[("g", g)]
            t, w0 = tb[g // 2], 16 * (g % 2)
            n = 16 - g % 2
            nc.vector.tensor_tensor(
                out=t[:, w0 + 1:w0 + 1 + n, 0:32],
                in0=chunks(glo[:, 0:32 * n]),
                in1=bias[:, 0:32].unsqueeze(1).to_broadcast([P, n, 32]),
                op=ALU.add,
            )
            nc.vector.tensor_tensor(
                out=t[:, w0:w0 + 16, 32:64],
                in0=chunks(ghi[:]),
                in1=bias[:, 32:64].unsqueeze(1).to_broadcast([P, 16, 32]),
                op=ALU.add,
            )

        def window_max(g):
            t, w0 = tb[g // 2], 16 * (g % 2)
            negm = sm.tile([P, 16], F32, name="negm", bufs=3)
            nc.vector.tensor_reduce(out=negm[:], in_=t[:, w0:w0 + 16, :], axis=AX.X, op=ALU.max, negate=True)
            st[("negm", g)] = negm

        def exps(g):
            t, w0 = tb[g // 2], 16 * (g % 2)
            negm = st[("negm", g)]
            h, c0 = g // 8, 16 * (g % 8)
            for w in range(16):
                nc.scalar.activation(
                    out=t[:, w0 + w, :],
                    in_=t[:, w0 + w, :],
                    func=ACT.Exp,
                    bias=negm[:, w:w + 1],
                    scale=1.0,
                    accum_out=den[h][:, c0 + w:c0 + w + 1],
                )

        def kv_evac(g):
            kvb = sm.tile([P, 256], F32, name="kvb", bufs=3)
            nc.scalar.copy(out=kvb[:], in_=st[("kv", g)][2][:])
            st[("kvb", g)] = kvb

        def mul(eng, view, other):
            eng.tensor_tensor(out=view, in0=view, in1=other, op=ALU.mult)

        def weigh(g):
            kla, khi, klb = st[("kv", g)]
            t, w0 = tb[g // 2], 16 * (g % 2)
            if not OFFLOAD:
                mul(nc.vector, t[:, w0 + 1:w0 + 16, 0:32], chunks(kla[:, 0:480]))
                if g % 2 == 0:
                    kvs = sm.tile([P, 32], F32, name="kvs")
                    nc.vector.tensor_copy(out=kvs[:], in_=kla[:, 480:512])
                    st[("kvs", g)] = kvs
                else:
                    mul(nc.vector, t[:, w0, 0:32], st[("kvs", g - 1)][:])
                mul(nc.vector, t[:, w0:w0 + 16, 32:64], chunks(khi[:]))
                return
            mul(nc.vector, t[:, w0 + 1:w0 + 9, 0:32], chunks(kla[:]))
            mul(nc.vector, t[:, w0:w0 + 16, 32:64], chunks(khi[:]))
            if g == NG - 1:
                mul(nc.vector, t[:, w0 + 9:w0 + 16, 0:32], chunks(klb[:, 0:224]))
                mul(nc.vector, t[:, w0, 0:32], st[("kvb", g - 1)][:, 224:256])

        def weigh_late(g):
            t, w0 = tb[g // 2], 16 * (g % 2)
            mul(nc.gpsimd, t[:, w0 + 9:w0 + 16, 0:32], chunks(st[("kvb", g)][:, 0:224]))
            if g % 2 == 1:
                mul(nc.gpsimd, t[:, w0, 0:32], st[("kvb", g - 1)][:, 224:256])

        def tree(g):
            t, w0 = tb[g // 2], 16 * (g % 2)
            n = 32
            while n >= LEFT:
                nc.gpsimd.tensor_tensor(
                    out=t[:, w0:w0 + 16, 0:n], in0=t[:, w0:w0 + 16, 0:n], in1=t[:, w0:w0 + 16, n:2 * n], op=ALU.add
                )
                n = n // 2

        def rest_sum(b, w0, nw, width):
            h, c0 = b // 4, 32 * (b % 4) + w0
            nc.vector.tensor_reduce(
                out=num[h][:, c0:c0 + nw], in_=tb[b][:, w0:w0 + nw, 0:width], axis=AX.X, op=ALU.add
            )

        def final_a(h):
            rden = sm.tile([P, P], F32, name="rden")
            nc.vector.reciprocal(out=rden[:], in_=den[h][:])
            pooled = sm.tile([P, P], F32, name="pooled")
            nc.vector.tensor_tensor(out=pooled[:], in0=num[h][:], in1=rden[:], op=ALU.mult)
            if h == 0:
                pt = mp.tile([P, P], F32, name="pt", tag="misc")
            else:
                pt = kp.tile([P, P], F32, name="pt", tag="klb")
            nc.tensor.transpose(pt[:], pooled[:], ident[:])
            st[("pt", h)] = pt

        def final_b(h):
            pt = st[("pt", h)]
            o = sm.tile([P, P], F32, name="o")
            nc.vector.tensor_copy(out=o[:, 0:64], in_=pt[:, 0:64])
            xr = pt[:, 64:128].rearrange("w (j e) -> w j e", e=2)
            y = sm.tile([P, 32, 2], F32, name="y")
            nc.vector.tensor_tensor(out=y[:], in0=xr, in1=cosT[:].unsqueeze(2).to_broadcast([P, 32, 2]), op=ALU.mult)
            z = sm.tile([P, 32, 2], F32, name="z")
            nc.vector.tensor_tensor(out=z[:, :, 0], in0=xr[:, :, 1], in1=ss[:, :, 0], op=ALU.mult)
            nc.vector.tensor_tensor(out=z[:, :, 1], in0=xr[:, :, 0], in1=ss[:, :, 1], op=ALU.mult)
            nc.vector.tensor_tensor(
                out=o[:, 64:128].rearrange("w (j e) -> w j e", e=2), in0=y[:], in1=z[:], op=ALU.add
            )
            nc.sync.dma_start(out=outr[128 * h:128 * h + 128, :], in_=o[:])

        def on(g):
            return 0 <= g < NG

        ctx.enter_context(tc.manual_schedule())
        transposes(0)
        evac(0)
        transposes(1)
        evac(1)
        quantise(0)
        w_regroup(0)
        gate_mm(0)
        transposes(2)
        evac(2)
        bias_add(0)
        quantise(1)
        gate_mm(1)
        transposes(3)
        evac(3)
        window_max(0)
        exps(0)
        transposes(4)
        bias_add(1)
        quantise(2)
        gate_mm(2)
        w_quantise(0)
        kv_mm(0)
        quantise(3)
        evac(4)
        kv_evac(0)
        weigh_late(0)
        window_max(1)
        exps(1)
        for k in range(2, NG + 2):
            if on(k + 3):
                transposes(k + 3)
            if on(k):
                bias_add(k)
            if k == 3:
                turns_a()
            if k == 4:
                turns_b()
            if on(k + 1):
                gate_mm(k + 1)
            if k >= 5 and k % 2 == 1:
                rest_sum((k - 5) // 2, 0, 32, LEFT)
            if on(k - 2):
                weigh(k - 2)
            if on(k - 2) and k - 2 < NG - 1:
                tree(k - 2)
            if on(k - 1):
                kv_mm(k - 1)
            if k == NG:
                final_a(0)
            if on(k + 2):
                quantise(k + 2)
            if on(k + 3):
                evac(k + 3)
            if OFFLOAD and on(k - 1) and k - 1 < NG - 1:
                kv_evac(k - 1)
                weigh_late(k - 1)
            if k == 5:
                reduce_angle()
            if on(k):
                window_max(k)
                exps(k)
            if k == NG - 1:
                sin_cos()
        cos_finish()
        rest_sum(7, 16, 16, 64)
        rest_sum(7, 0, 16, LEFT)
        final_a(1)
        final_b(0)
        final_b(1)
